import numpy as np
import ml_dtypes


def mxq(x, axis, fmt="e4m3"):
    dtype, down = {"e4m3": (ml_dtypes.float8_e4m3fn, 7), "e5m2": (ml_dtypes.float8_e5m2, 14)}[fmt]
    v = np.moveaxis(np.asarray(x, np.float32).astype(ml_dtypes.bfloat16).astype(np.float64), axis, -1)
    blocks = v.reshape(v.shape[:-1] + (-1, 32))
    amax = np.abs(blocks).max(-1, keepdims=True)
    byte = np.maximum(np.where(amax > 0, np.frexp(amax)[1] - 1 + 127, 0) - down, 1)
    scale = np.exp2(byte - 127.0)
    codes = (blocks / scale).astype(np.float32).astype(dtype).astype(np.float64)
    return np.moveaxis((codes * scale).reshape(v.shape), -1, axis)


WIDE = False


def mx_kscale(k):
    if not WIDE:
        return np.ones(k)
    levels = np.array([10, -10, 5, -5, 0])
    a = np.random.permutation(np.resize(levels, k // 512 * 4)).reshape(k // 512, 4)
    idx = np.arange(k)
    return np.exp2(a[idx // 512, idx % 128 // 32])


BF16 = ml_dtypes.bfloat16


def bf(x):
    return np.asarray(x, np.float32).astype(BF16)


def f64(x):
    return np.asarray(x).astype(np.float64)


E2M1 = np.array([0.0, 0.5, 1.0, 1.5, 2.0, 3.0, 4.0, 6.0, -0.0, -0.5, -1.0, -1.5, -2.0, -3.0, -4.0, -6.0])


def pack_weight(w, fmt):
    k, n = w.shape
    w = f64(bf(w)).reshape(k // 32, 32, n)
    amax = np.abs(w).max(1)
    if fmt == "e4m3":
        byte = np.frexp(amax)[1] - 1 + 127 - 7
    else:
        mant, ex = np.frexp(amax / 6.0)
        byte = np.where(mant > 0.5, ex, ex - 1) + 127
    byte = np.clip(np.where(amax > 0, byte, 1), 1, 254)
    scaled = (w * np.exp2(127.0 - byte)[:, None, :]).reshape(k, n).astype(np.float32)
    by_word = np.ascontiguousarray(scaled.reshape(k // 512, 128, 4, n).transpose(0, 1, 3, 2))
    if fmt == "e4m3":
        words = by_word.astype(ml_dtypes.float8_e4m3fn).view(np.uint8)
    else:
        c = by_word.astype(ml_dtypes.float4_e2m1fn).view(np.uint8) & 0xF
        words = c[..., 0::2] | (c[..., 1::2] << 4)
    return np.ascontiguousarray(words), np.ascontiguousarray(byte.astype(np.uint8).reshape(k // 512, 16, n))


def unpack_weight(words, scales, fmt):
    g, p, n, _ = words.shape
    if fmt == "e4m3":
        vals = np.ascontiguousarray(words).view(ml_dtypes.float8_e4m3fn).astype(np.float64)
    else:
        nib = np.empty((g, p, n, 4), np.uint8)
        nib[..., 0::2] = words & 0xF
        nib[..., 1::2] = words >> 4
        vals = E2M1[nib]
    vals = vals * np.repeat(np.exp2(scales.astype(np.float64) - 127.0), 8, axis=1)[..., None]
    return vals.transpose(0, 1, 3, 2).reshape(g * 512, n)

def pack4(w):
    words, scales = pack_weight(w, "e2m1")
    return words.reshape(words.shape[0], 128, -1), scales


def unpack4(words, scales):
    return unpack_weight(words.reshape(words.shape[0], 128, -1, 2), scales, "e2m1")


B, T, D, H, NUM_LAYERS = 2, 2048, 1024, 512, 3
EPS = 1e-8


def setup_inputs():
    s = mx_kscale(D)
    inv = bf(np.random.standard_normal((B, T, D)) * 0.5 * s)
    Wk = np.random.standard_normal((D, D)) * 2.0 / np.sqrt(D) / s[None, :]
    words, scales = pack4(np.ascontiguousarray(Wk.T))
    bk = bf(2.5 / np.sqrt(D) + 0.7 * np.random.standard_normal(D))
    return {"inv": inv,
            "Wk_words": words,
            "Wk_scales": scales,
            "bk": bk}


def reference(inv, Wk_words, Wk_scales, bk):
    flat = f64(inv).reshape(-1, D)
    out = (mxq(flat, 1, "e4m3") @ unpack4(Wk_words, Wk_scales)) + f64(bk)
    sqrtD = np.sqrt(D)
    S = out.sum(-1, keepdims=True)
    norms = np.sqrt((out * out).sum(-1, keepdims=True))
    c = out * S / (np.maximum(np.abs(out) * sqrtD, EPS) * np.maximum(norms, EPS))
    diff = np.abs(c[1:] - c[:-1]).sum(0)
    return np.broadcast_to(diff, (D, D)).copy()

@@ -1,0 +1,232 @@
+import math
+from contextlib import ExitStack
+
+import concourse.mybir as mybir
+from concourse.masks import make_identity
+
+F32 = mybir.dt.float32
+BF16 = mybir.dt.bfloat16
+U8 = mybir.dt.uint8
+U32 = mybir.dt.uint32
+I32 = mybir.dt.int32
+FP8X4 = mybir.dt.float8_e4m3fn_x4
+FP4X4 = mybir.dt.float4_e2m1fn_x4
+ALU = mybir.AluOpType
+ACT = mybir.ActivationFunctionType
+AXIS = mybir.AxisListType
+
+P = 128
+TOKENS = 4096
+D = 1024
+K_PASS = 4 * P
+PASSES = D // K_PASS
+BANK = 512
+HALVES = D // BANK
+ROUNDS = TOKENS // P
+TILES = ROUNDS + 1
+D_TILES = D // P
+GROUP = BANK // P
+EPS = 1e-8
+DELTA = EPS / math.sqrt(D)
+
+FLOPS = 2 * TOKENS * D * D
+
+
+def tile_dispatcher_pa_t_kernel(tc, inv, Wk_words, Wk_scales, bk, out):
+    nc = tc.nc
+    flat = inv.flatten_outer_dims()
+    by_partition = flat.rearrange("(p t) k -> p t k", t=ROUNDS)
+    next_first = flat[ROUNDS:TOKENS, :].rearrange("(p t) k -> p t k", t=ROUNDS)
+
+    with ExitStack() as stack:
+        keep = stack.enter_context(tc.tile_pool(name="keep", bufs=1))
+        stage = stack.enter_context(tc.tile_pool(name="stage", bufs=3))
+        waste = stack.enter_context(tc.tile_pool(name="waste", bufs=2))
+        waiting = stack.enter_context(tc.tile_pool(name="waiting", bufs=6))
+        turning = stack.enter_context(tc.tile_pool(name="turning", bufs=10))
+        psum = stack.enter_context(tc.psum_pool(name="psum", bufs=2))
+        stack.enter_context(tc.manual_schedule())
+
+        x_pairs = []
+        for s in range(ROUNDS // 2):
+            x_pair = keep.tile([P, 2, D], BF16, name="x_pair%d" % s)
+            x_pairs.append(x_pair)
+        x_wrap = keep.tile([P, D], BF16, name="x_wrap")
+        w_words = keep.tile([P, PASSES, 2 * D], U8, name="w_words", align_bytes=64)
+        w_planes = keep.tile([P, PASSES, D], U8, name="w_planes", align_bytes=64)
+        bias = keep.tile([P, D], BF16, name="bias")
+
+        nc.vector.memset(w_planes[:].bitcast(I32), 0)
+        nc.scalar.dma_start(out=bias[:], in_=bk.partition_broadcast(P))
+        nc.sync.dma_start(out=x_pairs[0][:], in_=by_partition[:, 0:2, :])
+        nc.sync.dma_start(
+            out=w_words[:].bitcast(I32), in_=Wk_words.rearrange("g p b -> p g b").bitcast(I32)
+        )
+        for quadrant in range(4):
+            nc.sync.dma_start(
+                out=w_planes[32 * quadrant : 32 * quadrant + 4, :, :].bitcast(I32),
+                in_=Wk_scales[:, 4 * quadrant : 4 * quadrant + 4, :].rearrange("g r n -> r g n").bitcast(I32),
+            )
+        for s in range(1, ROUNDS // 2):
+            nc.sync.dma_start(out=x_pairs[s][:], in_=by_partition[:, 2 * s : 2 * s + 2, :])
+        nc.sync.dma_start(out=x_wrap[0 : P - 1, :], in_=next_first[:, 0, :])
+        nc.sync.dma_start(out=x_wrap[P - 1 : P, :], in_=flat[TOKENS - 1 : TOKENS, :])
+
+        ident = keep.tile([P, P], F32, name="ident")
+        make_identity(nc, ident[:])
+        neg_half = keep.tile([P, GROUP], F32, name="neg_half")
+        nc.gpsimd.memset(neg_half[:], -0.5)
+
+        row_sums = keep.tile([P, HALVES, TILES], F32, name="row_sums")
+        norm_sq = keep.tile([P, TILES], F32, name="norm_sq")
+        totals = keep.tile([P, TILES], F32, name="totals")
+        floored = keep.tile([P, TILES], F32, name="floored")
+        inv_norm = keep.tile([P, TILES], F32, name="inv_norm")
+        scales = keep.tile([P, TILES], F32, name="scales")
+        abs_sums = keep.tile([P, D_TILES, ROUNDS // GROUP], F32, name="abs_sums")
+
+        grouped, codes, planes, acc, lin, clamped, signed = {}, {}, {}, {}, {}, {}, {}
+
+        def turn_tokens(t):
+            x_tile = x_pairs[t // 2][:, t % 2, :] if t < ROUNDS else x_wrap[:]
+            x_words = x_tile.bitcast(F32)
+            xt = psum.tile([P, 2 * PASSES, P], F32, name="xt")
+            for g in range(PASSES):
+                for u in range(2):
+                    nc.tensor.transpose(
+                        xt[:, 2 * g + u, :], x_words[:, 256 * g + u : 256 * (g + 1) : 2], ident[:]
+                    )
+            grouped[t] = stage.tile([P, PASSES, P, 4], BF16, name="grouped", align_bytes=64)
+            nc.scalar.copy(
+                out=grouped[t][:].bitcast(F32), in_=xt[:].rearrange("p (g u) r -> p g r u", u=2)
+            )
+
+        def quantise(t):
+            codes[t] = stage.tile([P, PASSES * P], U32, name="codes", align_bytes=64)
+            planes[t] = stage.tile([P, PASSES * P], U8, name="planes", align_bytes=64)
+            nc.vector.quantize_mx(
+                out=codes[t][:].bitcast(FP8X4),
+                scales=planes[t][:],
+                in_=grouped[t][:].rearrange("p g r t -> p (g r t)"),
+            )
+
+        def multiply(t):
+            for h in range(HALVES):
+                acc[t, h] = psum.tile([P, BANK], F32, name="acc%d" % h)
+                for g in range(PASSES):
+                    nc.tensor.matmul_mx(
+                        out=acc[t, h][:],
+                        lhsT=codes[t][:, g * P : (g + 1) * P].bitcast(FP8X4),
+                        lhsT_scale=planes[t][:, g * P : (g + 1) * P],
+                        rhs=w_words[:, g, 2 * BANK * h : 2 * BANK * (h + 1)].bitcast(FP4X4),
+                        rhs_scale=w_planes[:, g, BANK * h : BANK * (h + 1)],
+                        start=(g == 0),
+                        stop=(g == PASSES - 1),
+                    )
+
+        def add_bias(t):
+            lin[t] = stage.tile([P, D], F32, name="lin")
+            for h in range(HALVES):
+                nc.vector.scalar_tensor_tensor(
+                    out=lin[t][:, BANK * h : BANK * (h + 1)],
+                    in0=acc[t, h][:],
+                    scalar=1.0,
+                    in1=bias[:, BANK * h : BANK * (h + 1)],
+                    op0=ALU.mult,
+                    op1=ALU.add,
+                    accum_out=row_sums[:, h, t : t + 1],
+                )
+
+        def clamp_and_square(t):
+            clamped[t] = waiting.tile([P, D], F32, name="clamped")
+            nc.vector.tensor_scalar(
+                out=clamped[t][:], in0=lin[t][:], scalar1=-DELTA, scalar2=DELTA, op0=ALU.max, op1=ALU.min
+            )
+            squares = waste.tile([P, D], F32, name="squares")
+            nc.scalar.activation(
+                out=squares[:], in_=lin[t][:], func=ACT.Square, accum_out=norm_sq[:, t : t + 1]
+            )
+
+        def row_scales(first, count):
+            cols = slice(first, first + count)
+            nc.gpsimd.tensor_tensor(
+                out=totals[:, cols], in0=row_sums[:, 0, cols], in1=row_sums[:, 1, cols], op=ALU.add
+            )
+            nc.gpsimd.tensor_scalar(
+                out=floored[:, cols], in0=norm_sq[:, cols], scalar1=EPS * EPS, scalar2=EPS * EPS,
+                op0=ALU.max, op1=ALU.mult,
+            )
+            nc.gpsimd.tensor_tensor(
+                out=inv_norm[:, cols], in0=floored[:, cols], in1=neg_half[:, 0:count], op=ALU.pow
+            )
+            nc.gpsimd.tensor_tensor(
+                out=scales[:, cols], in0=totals[:, cols], in1=inv_norm[:, cols], op=ALU.mult
+            )
+
+        def scale_rows(t):
+            signed[t] = turning.tile([P, D], F32, name="signed")
+            nc.vector.tensor_scalar(
+                out=signed[t][:],
+                in0=clamped[t][:],
+                scalar1=scales[:, t : t + 1],
+                scalar2=(1.0 if t % 2 == 0 else -1.0),
+                op0=ALU.mult,
+                op1=ALU.mult,
+            )
+
+        def sum_differences(q, m):
+            turned = psum.tile([P, GROUP, P], F32, name="turned")
+            for i in range(GROUP):
+                for side in range(2):
+                    nc.tensor.matmul(
+                        out=turned[:, i, :],
+                        lhsT=signed[GROUP * q + i + side][:, m * P : (m + 1) * P],
+                        rhs=ident[:],
+                        is_transpose=True,
+                        start=(side == 0),
+                        stop=(side == 1),
+                    )
+            magnitudes = waste.tile([P, GROUP, P], F32, name="magnitudes")
+            nc.scalar.activation(
+                out=magnitudes[:], in_=turned[:], func=ACT.Abs, accum_out=abs_sums[:, m, q : q + 1]
+            )
+
+        for k in range(TILES + 10):
+            if k < TILES:
+                turn_tokens(k)
+            if 0 <= k - 1 < TILES:
+                quantise(k - 1)
+                multiply(k - 1)
+            if 0 <= k - 2 < TILES:
+                add_bias(k - 2)
+                clamp_and_square(k - 2)
+                if (k - 2) % GROUP == GROUP - 1:
+                    row_scales(k - 2 - (GROUP - 1), GROUP)
+                if k - 2 == TILES - 1:
+                    row_scales(k - 2, 1)
+            if 0 <= k - 6 < TILES:
+                scale_rows(k - 6)
+            if 0 <= k - 11 < ROUNDS:
+                for bank in (2 * (k - 11), 2 * (k - 11) + 1):
+                    sum_differences(bank // D_TILES, bank % D_TILES)
+
+        diff_t = keep.tile([P, D_TILES], F32, name="diff_t")
+        nc.vector.tensor_reduce(out=diff_t[:], in_=abs_sums[:], axis=AXIS.X, op=ALU.add)
+        loss_rows = keep.tile([P, D], F32, name="loss_rows")
+        for h in range(HALVES):
+            spread = psum.tile([P, BANK], F32, name="acc%d" % h)
+            for i in range(BANK // P):
+                m = h * (BANK // P) + i
+                nc.tensor.matmul(
+                    out=spread[:, i * P : (i + 1) * P],
+                    lhsT=diff_t[:, m : m + 1].to_broadcast([P, P]),
+                    rhs=ident[:],
+                    start=True,
+                    stop=True,
+                )
+            if h == 0:
+                nc.vector.tensor_copy(out=loss_rows[:, 0:BANK], in_=spread[:])
+            else:
+                nc.scalar.copy(out=loss_rows[:, BANK : 2 * BANK], in_=spread[:])
+        for a in range(D // P):
+            nc.sync.dma_start(out=out[a * P : (a + 1) * P, :], in_=loss_rows[:])

@@ -42,8 +42,9 @@ def tile_dispatcher_pa_t_kernel(tc, inv, Wk_words, Wk_scales, bk, out):
         keep = stack.enter_context(tc.tile_pool(name="keep", bufs=1))
         stage = stack.enter_context(tc.tile_pool(name="stage", bufs=3))
         waste = stack.enter_context(tc.tile_pool(name="waste", bufs=2))
-        waiting = stack.enter_context(tc.tile_pool(name="waiting", bufs=6))
-        turning = stack.enter_context(tc.tile_pool(name="turning", bufs=10))
+        waiting = stack.enter_context(tc.tile_pool(name="waiting", bufs=8))
+        ready = stack.enter_context(tc.tile_pool(name="ready", bufs=3))
+        turning = stack.enter_context(tc.tile_pool(name="turning", bufs=2))
         psum = stack.enter_context(tc.psum_pool(name="psum", bufs=2))
         stack.enter_context(tc.manual_schedule())
 
@@ -85,7 +86,7 @@ def tile_dispatcher_pa_t_kernel(tc, inv, Wk_words, Wk_scales, bk, out):
         scales = keep.tile([P, TILES], F32, name="scales")
         abs_sums = keep.tile([P, D_TILES, ROUNDS // GROUP], F32, name="abs_sums")
 
-        grouped, codes, planes, acc, lin, clamped, signed = {}, {}, {}, {}, {}, {}, {}
+        grouped, codes, planes, acc, lin, clamped, scaled, diffs = {}, {}, {}, {}, {}, {}, {}, {}
 
         def turn_tokens(t):
             x_tile = x_pairs[t // 2][:, t % 2, :] if t < ROUNDS else x_wrap[:]
@@ -163,35 +164,40 @@ def tile_dispatcher_pa_t_kernel(tc, inv, Wk_words, Wk_scales, bk, out):
                 out=scales[:, cols], in0=totals[:, cols], in1=inv_norm[:, cols], op=ALU.mult
             )
 
-        def scale_rows(t):
-            signed[t] = turning.tile([P, D], F32, name="signed")
-            nc.vector.tensor_scalar(
-                out=signed[t][:],
-                in0=clamped[t][:],
-                scalar1=scales[:, t : t + 1],
-                scalar2=(1.0 if t % 2 == 0 else -1.0),
+        def scale_even(t):
+            scaled[t] = ready.tile([P, D], F32, name="scaled")
+            if t % 4 == 0:
+                nc.vector.tensor_scalar(
+                    out=scaled[t][:], in0=clamped[t][:], scalar1=scales[:, t : t + 1], scalar2=None, op0=ALU.mult
+                )
+            else:
+                nc.scalar.activation(
+                    out=scaled[t][:], in_=clamped[t][:], func=ACT.Copy, scale=scales[:, t : t + 1]
+                )
+
+        def difference(j):
+            odd, even = (j, j + 1) if j % 2 == 1 else (j + 1, j)
+            if j % GROUP == 0:
+                diffs[j // GROUP] = turning.tile([P, GROUP, D], F32, name="diffs")
+            nc.vector.scalar_tensor_tensor(
+                out=diffs[j // GROUP][:, j % GROUP, :],
+                in0=clamped[odd][:],
+                scalar=scales[:, odd : odd + 1],
+                in1=scaled[even][:],
                 op0=ALU.mult,
-                op1=ALU.mult,
+                op1=ALU.subtract,
             )
 
         def sum_differences(q, m):
             turned = psum.tile([P, GROUP, P], F32, name="turned")
             for i in range(GROUP):
-                for side in range(2):
-                    nc.tensor.matmul(
-                        out=turned[:, i, :],
-                        lhsT=signed[GROUP * q + i + side][:, m * P : (m + 1) * P],
-                        rhs=ident[:],
-                        is_transpose=True,
-                        start=(side == 0),
-                        stop=(side == 1),
-                    )
+                nc.tensor.transpose(turned[:, i, :], diffs[q][:, i, m * P : (m + 1) * P], ident[:])
             magnitudes = waste.tile([P, GROUP, P], F32, name="magnitudes")
             nc.scalar.activation(
                 out=magnitudes[:], in_=turned[:], func=ACT.Abs, accum_out=abs_sums[:, m, q : q + 1]
             )
 
-        for k in range(TILES + 10):
+        for k in range(TILES + 11):
             if k < TILES:
                 turn_tokens(k)
             if 0 <= k - 1 < TILES:
@@ -204,10 +210,12 @@ def tile_dispatcher_pa_t_kernel(tc, inv, Wk_words, Wk_scales, bk, out):
                     row_scales(k - 2 - (GROUP - 1), GROUP)
                 if k - 2 == TILES - 1:
                     row_scales(k - 2, 1)
-            if 0 <= k - 6 < TILES:
-                scale_rows(k - 6)
-            if 0 <= k - 11 < ROUNDS:
-                for bank in (2 * (k - 11), 2 * (k - 11) + 1):
+            if 0 <= k - 6 < TILES and (k - 6) % 2 == 0:
+                scale_even(k - 6)
+            if 0 <= k - 8 < ROUNDS:
+                difference(k - 8)
+            if 0 <= k - 12 < ROUNDS:
+                for bank in (2 * (k - 12), 2 * (k - 12) + 1):
                     sum_differences(bank // D_TILES, bank % D_TILES)
 
         diff_t = keep.tile([P, D_TILES], F32, name="diff_t")

@@ -42,9 +42,8 @@ def tile_dispatcher_pa_t_kernel(tc, inv, Wk_words, Wk_scales, bk, out):
         keep = stack.enter_context(tc.tile_pool(name="keep", bufs=1))
         stage = stack.enter_context(tc.tile_pool(name="stage", bufs=3))
         waste = stack.enter_context(tc.tile_pool(name="waste", bufs=2))
-        waiting = stack.enter_context(tc.tile_pool(name="waiting", bufs=8))
-        ready = stack.enter_context(tc.tile_pool(name="ready", bufs=3))
-        turning = stack.enter_context(tc.tile_pool(name="turning", bufs=2))
+        waiting = stack.enter_context(tc.tile_pool(name="waiting", bufs=3))
+        turning = stack.enter_context(tc.tile_pool(name="turning", bufs=10))
         psum = stack.enter_context(tc.psum_pool(name="psum", bufs=2))
         stack.enter_context(tc.manual_schedule())
 
@@ -75,18 +74,19 @@ def tile_dispatcher_pa_t_kernel(tc, inv, Wk_words, Wk_scales, bk, out):
 
         ident = keep.tile([P, P], F32, name="ident")
         make_identity(nc, ident[:])
-        neg_half = keep.tile([P, GROUP], F32, name="neg_half")
+        neg_half = keep.tile([P, 1], F32, name="neg_half")
         nc.gpsimd.memset(neg_half[:], -0.5)
 
         row_sums = keep.tile([P, HALVES, TILES], F32, name="row_sums")
         norm_sq = keep.tile([P, TILES], F32, name="norm_sq")
-        totals = keep.tile([P, TILES], F32, name="totals")
         floored = keep.tile([P, TILES], F32, name="floored")
         inv_norm = keep.tile([P, TILES], F32, name="inv_norm")
         scales = keep.tile([P, TILES], F32, name="scales")
-        abs_sums = keep.tile([P, D_TILES, ROUNDS // GROUP], F32, name="abs_sums")
+        groups = [list(range(j, j + GROUP)) for j in range(0, ROUNDS - GROUP, GROUP)]
+        groups.extend([[ROUNDS - 4, ROUNDS - 3], [ROUNDS - 2, ROUNDS - 1]])
+        abs_sums = keep.tile([P, D_TILES, len(groups)], F32, name="abs_sums")
 
-        grouped, codes, planes, acc, lin, clamped, scaled, diffs = {}, {}, {}, {}, {}, {}, {}, {}
+        grouped, codes, planes, acc, lin, clamped, signed = {}, {}, {}, {}, {}, {}, {}
 
         def turn_tokens(t):
             x_tile = x_pairs[t // 2][:, t % 2, :] if t < ROUNDS else x_wrap[:]
@@ -148,56 +148,53 @@ def tile_dispatcher_pa_t_kernel(tc, inv, Wk_words, Wk_scales, bk, out):
                 out=squares[:], in_=lin[t][:], func=ACT.Square, accum_out=norm_sq[:, t : t + 1]
             )
 
-        def row_scales(first, count):
-            cols = slice(first, first + count)
-            nc.gpsimd.tensor_tensor(
-                out=totals[:, cols], in0=row_sums[:, 0, cols], in1=row_sums[:, 1, cols], op=ALU.add
-            )
+        def row_scale(t):
+            col = slice(t, t + 1)
             nc.gpsimd.tensor_scalar(
-                out=floored[:, cols], in0=norm_sq[:, cols], scalar1=EPS * EPS, scalar2=EPS * EPS,
+                out=floored[:, col], in0=norm_sq[:, col], scalar1=EPS * EPS, scalar2=EPS * EPS,
                 op0=ALU.max, op1=ALU.mult,
             )
-            nc.gpsimd.tensor_tensor(
-                out=inv_norm[:, cols], in0=floored[:, cols], in1=neg_half[:, 0:count], op=ALU.pow
-            )
-            nc.gpsimd.tensor_tensor(
-                out=scales[:, cols], in0=totals[:, cols], in1=inv_norm[:, cols], op=ALU.mult
+            nc.gpsimd.tensor_tensor(out=inv_norm[:, col], in0=floored[:, col], in1=neg_half[:], op=ALU.pow)
+            nc.gpsimd.tensor_scalar(
+                out=scales[:, col], in0=row_sums[:, 0, col], scalar1=row_sums[:, 1, col], scalar2=inv_norm[:, col],
+                op0=ALU.add, op1=ALU.mult,
             )
 
-        def scale_even(t):
-            scaled[t] = ready.tile([P, D], F32, name="scaled")
-            if t % 4 == 0:
-                nc.vector.tensor_scalar(
-                    out=scaled[t][:], in0=clamped[t][:], scalar1=scales[:, t : t + 1], scalar2=None, op0=ALU.mult
-                )
-            else:
-                nc.scalar.activation(
-                    out=scaled[t][:], in_=clamped[t][:], func=ACT.Copy, scale=scales[:, t : t + 1]
-                )
-
-        def difference(j):
-            odd, even = (j, j + 1) if j % 2 == 1 else (j + 1, j)
-            if j % GROUP == 0:
-                diffs[j // GROUP] = turning.tile([P, GROUP, D], F32, name="diffs")
-            nc.vector.scalar_tensor_tensor(
-                out=diffs[j // GROUP][:, j % GROUP, :],
-                in0=clamped[odd][:],
-                scalar=scales[:, odd : odd + 1],
-                in1=scaled[even][:],
+        def scale_rows(t):
+            signed[t] = turning.tile([P, D], F32, name="signed")
+            nc.vector.tensor_scalar(
+                out=signed[t][:],
+                in0=clamped[t][:],
+                scalar1=scales[:, t : t + 1],
+                scalar2=(1.0 if t % 2 == 0 else -1.0),
                 op0=ALU.mult,
-                op1=ALU.subtract,
+                op1=ALU.mult,
             )
 
         def sum_differences(q, m):
+            width = len(groups[q])
             turned = psum.tile([P, GROUP, P], F32, name="turned")
-            for i in range(GROUP):
-                nc.tensor.transpose(turned[:, i, :], diffs[q][:, i, m * P : (m + 1) * P], ident[:])
+            for i, j in enumerate(groups[q]):
+                for side in range(2):
+                    nc.tensor.matmul(
+                        out=turned[:, i, :],
+                        lhsT=signed[j + side][:, m * P : (m + 1) * P],
+                        rhs=ident[:],
+                        is_transpose=True,
+                        start=(side == 0),
+                        stop=(side == 1),
+                    )
             magnitudes = waste.tile([P, GROUP, P], F32, name="magnitudes")
             nc.scalar.activation(
-                out=magnitudes[:], in_=turned[:], func=ACT.Abs, accum_out=abs_sums[:, m, q : q + 1]
+                out=magnitudes[:, 0:width, :],
+                in_=turned[:, 0:width, :],
+                func=ACT.Abs,
+                accum_out=abs_sums[:, m, q : q + 1],
             )
 
-        for k in range(TILES + 11):
+        in_line = []
+        k = 0
+        while k < TILES + 3 or in_line:
             if k < TILES:
                 turn_tokens(k)
             if 0 <= k - 1 < TILES:
@@ -206,17 +203,16 @@ def tile_dispatcher_pa_t_kernel(tc, inv, Wk_words, Wk_scales, bk, out):
             if 0 <= k - 2 < TILES:
                 add_bias(k - 2)
                 clamp_and_square(k - 2)
-                if (k - 2) % GROUP == GROUP - 1:
-                    row_scales(k - 2 - (GROUP - 1), GROUP)
-                if k - 2 == TILES - 1:
-                    row_scales(k - 2, 1)
-            if 0 <= k - 6 < TILES and (k - 6) % 2 == 0:
-                scale_even(k - 6)
-            if 0 <= k - 8 < ROUNDS:
-                difference(k - 8)
-            if 0 <= k - 12 < ROUNDS:
-                for bank in (2 * (k - 12), 2 * (k - 12) + 1):
-                    sum_differences(bank // D_TILES, bank % D_TILES)
+                row_scale(k - 2)
+            if 0 <= k - 3 < TILES:
+                scale_rows(k - 3)
+                for q in range(len(groups)):
+                    if groups[q][-1] + 1 == k - 3:
+                        in_line.extend([(q, m) for m in range(D_TILES)])
+            for q, m in in_line[0:2]:
+                sum_differences(q, m)
+            in_line = in_line[2:]
+            k += 1
 
         diff_t = keep.tile([P, D_TILES], F32, name="diff_t")
         nc.vector.tensor_reduce(out=diff_t[:], in_=abs_sums[:], axis=AXIS.X, op=ALU.add)
@@ -225,12 +221,8 @@ def tile_dispatcher_pa_t_kernel(tc, inv, Wk_words, Wk_scales, bk, out):
             spread = psum.tile([P, BANK], F32, name="acc%d" % h)
             for i in range(BANK // P):
                 m = h * (BANK // P) + i
-                nc.tensor.matmul(
-                    out=spread[:, i * P : (i + 1) * P],
-                    lhsT=diff_t[:, m : m + 1].to_broadcast([P, P]),
-                    rhs=ident[:],
-                    start=True,
-                    stop=True,
+                nc.tensor.transpose(
+                    spread[:, i * P : (i + 1) * P], diff_t[:, m : m + 1].to_broadcast([P, P]), ident[:]
                 )
             if h == 0:
                 nc.vector.tensor_copy(out=loss_rows[:, 0:BANK], in_=spread[:])

@@ -23,7 +23,7 @@ PASSES = D // K_PASS
 BANK = 512
 HALVES = D // BANK
 ROUNDS = TOKENS // P
-TILES = ROUNDS + 1
+TILES = ROUNDS
 D_TILES = D // P
 GROUP = BANK // P
 EPS = 1e-8
@@ -36,7 +36,6 @@ def tile_dispatcher_pa_t_kernel(tc, inv, Wk_words, Wk_scales, bk, out):
     nc = tc.nc
     flat = inv.flatten_outer_dims()
     by_partition = flat.rearrange("(p t) k -> p t k", t=ROUNDS)
-    next_first = flat[ROUNDS:TOKENS, :].rearrange("(p t) k -> p t k", t=ROUNDS)
 
     with ExitStack() as stack:
         keep = stack.enter_context(tc.tile_pool(name="keep", bufs=1))
@@ -51,7 +50,6 @@ def tile_dispatcher_pa_t_kernel(tc, inv, Wk_words, Wk_scales, bk, out):
         for s in range(ROUNDS // 2):
             x_pair = keep.tile([P, 2, D], BF16, name="x_pair%d" % s)
             x_pairs.append(x_pair)
-        x_wrap = keep.tile([P, D], BF16, name="x_wrap")
         w_words = keep.tile([P, PASSES, 2 * D], U8, name="w_words", align_bytes=64)
         w_planes = keep.tile([P, PASSES, D], U8, name="w_planes", align_bytes=64)
         bias = keep.tile([P, D], BF16, name="bias")
@@ -69,11 +67,13 @@ def tile_dispatcher_pa_t_kernel(tc, inv, Wk_words, Wk_scales, bk, out):
             )
         for s in range(1, ROUNDS // 2):
             nc.sync.dma_start(out=x_pairs[s][:], in_=by_partition[:, 2 * s : 2 * s + 2, :])
-        nc.sync.dma_start(out=x_wrap[0 : P - 1, :], in_=next_first[:, 0, :])
-        nc.sync.dma_start(out=x_wrap[P - 1 : P, :], in_=flat[TOKENS - 1 : TOKENS, :])
 
         ident = keep.tile([P, P], F32, name="ident")
         make_identity(nc, ident[:])
+        next_row = keep.tile([P, P], F32, name="next_row")
+        nc.vector.tensor_copy(out=next_row[:, 0 : P - 1], in_=ident[:, 1:P])
+        nc.vector.tensor_copy(out=next_row[:, P - 1 : P], in_=ident[:, 0:1])
+        first_signed = keep.tile([P, D], F32, name="first_signed")
         neg_half = keep.tile([P, 1], F32, name="neg_half")
         nc.gpsimd.memset(neg_half[:], -0.5)
 
@@ -89,7 +89,7 @@ def tile_dispatcher_pa_t_kernel(tc, inv, Wk_words, Wk_scales, bk, out):
         grouped, codes, planes, acc, lin, clamped, signed = {}, {}, {}, {}, {}, {}, {}
 
         def turn_tokens(t):
-            x_tile = x_pairs[t // 2][:, t % 2, :] if t < ROUNDS else x_wrap[:]
+            x_tile = x_pairs[t // 2][:, t % 2, :]
             x_words = x_tile.bitcast(F32)
             xt = psum.tile([P, 2 * PASSES, P], F32, name="xt")
             for g in range(PASSES):
@@ -161,7 +161,10 @@ def tile_dispatcher_pa_t_kernel(tc, inv, Wk_words, Wk_scales, bk, out):
             )
 
         def scale_rows(t):
-            signed[t] = turning.tile([P, D], F32, name="signed")
+            if t == 0:
+                signed[t] = first_signed
+            else:
+                signed[t] = turning.tile([P, D], F32, name="signed")
             nc.vector.tensor_scalar(
                 out=signed[t][:],
                 in0=clamped[t][:],
@@ -172,22 +175,23 @@ def tile_dispatcher_pa_t_kernel(tc, inv, Wk_words, Wk_scales, bk, out):
             )
 
         def sum_differences(q, m):
-            width = len(groups[q])
-            turned = psum.tile([P, GROUP, P], F32, name="turned")
+            turned = psum.tile([P, GROUP * P], F32, name="turned")
             for i, j in enumerate(groups[q]):
                 for side in range(2):
+                    wraps = j + side == TILES
                     nc.tensor.matmul(
-                        out=turned[:, i, :],
-                        lhsT=signed[j + side][:, m * P : (m + 1) * P],
-                        rhs=ident[:],
+                        out=turned[:, i * P : (i + 1) * P],
+                        lhsT=signed[0 if wraps else j + side][:, m * P : (m + 1) * P],
+                        rhs=(next_row[:] if wraps else ident[:]),
                         is_transpose=True,
                         start=(side == 0),
                         stop=(side == 1),
                     )
-            magnitudes = waste.tile([P, GROUP, P], F32, name="magnitudes")
+            width = len(groups[q]) * P - (1 if groups[q][-1] == ROUNDS - 1 else 0)
+            magnitudes = waste.tile([P, GROUP * P], F32, name="magnitudes")
             nc.scalar.activation(
-                out=magnitudes[:, 0:width, :],
-                in_=turned[:, 0:width, :],
+                out=magnitudes[:, 0:width],
+                in_=turned[:, 0:width],
                 func=ACT.Abs,
                 accum_out=abs_sums[:, m, q : q + 1],
             )
@@ -207,7 +211,7 @@ def tile_dispatcher_pa_t_kernel(tc, inv, Wk_words, Wk_scales, bk, out):
             if 0 <= k - 3 < TILES:
                 scale_rows(k - 3)
                 for q in range(len(groups)):
-                    if groups[q][-1] + 1 == k - 3:
+                    if min(groups[q][-1] + 1, TILES - 1) == k - 3:
                         in_line.extend([(q, m) for m in range(D_TILES)])
             for q, m in in_line[0:2]:
                 sum_differences(q, m)

@@ -42,7 +42,7 @@ def tile_dispatcher_pa_t_kernel(tc, inv, Wk_words, Wk_scales, bk, out):
         stage = stack.enter_context(tc.tile_pool(name="stage", bufs=3))
         waste = stack.enter_context(tc.tile_pool(name="waste", bufs=2))
         waiting = stack.enter_context(tc.tile_pool(name="waiting", bufs=3))
-        turning = stack.enter_context(tc.tile_pool(name="turning", bufs=10))
+        turning = stack.enter_context(tc.tile_pool(name="turning", bufs=20))
         psum = stack.enter_context(tc.psum_pool(name="psum", bufs=2))
         stack.enter_context(tc.manual_schedule())
 
@@ -174,8 +174,8 @@ def tile_dispatcher_pa_t_kernel(tc, inv, Wk_words, Wk_scales, bk, out):
                 op1=ALU.mult,
             )
 
-        def sum_differences(q, m):
-            turned = psum.tile([P, GROUP * P], F32, name="turned")
+        def sum_differences(q, m, bank="turned"):
+            turned = psum.tile([P, GROUP * P], F32, name=bank)
             for i, j in enumerate(groups[q]):
                 for side in range(2):
                     wraps = j + side == TILES
@@ -196,9 +196,8 @@ def tile_dispatcher_pa_t_kernel(tc, inv, Wk_words, Wk_scales, bk, out):
                 accum_out=abs_sums[:, m, q : q + 1],
             )
 
-        in_line = []
-        k = 0
-        while k < TILES + 3 or in_line:
+        first_line, second_line = [], []
+        for k in range(TILES + 3):
             if k < TILES:
                 turn_tokens(k)
             if 0 <= k - 1 < TILES:
@@ -212,25 +211,50 @@ def tile_dispatcher_pa_t_kernel(tc, inv, Wk_words, Wk_scales, bk, out):
                 scale_rows(k - 3)
                 for q in range(len(groups)):
                     if min(groups[q][-1] + 1, TILES - 1) == k - 3:
-                        in_line.extend([(q, m) for m in range(D_TILES)])
-            for q, m in in_line[0:2]:
-                sum_differences(q, m)
-            in_line = in_line[2:]
-            k += 1
+                        first_line.extend([(q, m) for m in range(0, D_TILES // 2)])
+                        second_line.extend([(q, m) for m in range(D_TILES // 2, D_TILES)])
+            for turn in range(2 - k % 2):
+                if first_line:
+                    sum_differences(*first_line[0])
+                    first_line = first_line[1:]
+                elif second_line:
+                    sum_differences(*second_line[0])
+                    second_line = second_line[1:]
 
         diff_t = keep.tile([P, D_TILES], F32, name="diff_t")
-        nc.vector.tensor_reduce(out=diff_t[:], in_=abs_sums[:], axis=AXIS.X, op=ALU.add)
         loss_rows = keep.tile([P, D], F32, name="loss_rows")
-        for h in range(HALVES):
-            spread = psum.tile([P, BANK], F32, name="acc%d" % h)
-            for i in range(BANK // P):
-                m = h * (BANK // P) + i
+
+        def total(m0, m1):
+            nc.vector.tensor_reduce(out=diff_t[:, m0:m1], in_=abs_sums[:, m0:m1, :], axis=AXIS.X, op=ALU.add)
+
+        def spread_and_store(m0, m1):
+            spread = psum.tile([P, BANK], F32, name="turned")
+            for m in range(m0, m1):
                 nc.tensor.transpose(
-                    spread[:, i * P : (i + 1) * P], diff_t[:, m : m + 1].to_broadcast([P, P]), ident[:]
+                    spread[:, (m - m0) * P : (m - m0 + 1) * P], diff_t[:, m : m + 1].to_broadcast([P, P]), ident[:]
                 )
-            if h == 0:
-                nc.vector.tensor_copy(out=loss_rows[:, 0:BANK], in_=spread[:])
-            else:
-                nc.scalar.copy(out=loss_rows[:, BANK : 2 * BANK], in_=spread[:])
-        for a in range(D // P):
-            nc.sync.dma_start(out=out[a * P : (a + 1) * P, :], in_=loss_rows[:])
+            nc.vector.tensor_copy(out=loss_rows[:, m0 * P : m1 * P], in_=spread[:, 0 : (m1 - m0) * P])
+            for a in range(D // P):
+                nc.sync.dma_start(out=out[a * P : (a + 1) * P, m0 * P : m1 * P], in_=loss_rows[:, m0 * P : m1 * P])
+
+        banks = ["xt", "acc0", "acc1", "turned"]
+        count = 0
+        for q, m in first_line:
+            sum_differences(q, m, banks[count % 4])
+            count += 1
+        total(0, 4)
+        third = [b for b in second_line if b[1] < 6]
+        fourth = [b for b in second_line if b[1] >= 6]
+        for i, b in enumerate(third):
+            if i == 2:
+                spread_and_store(0, 4)
+            sum_differences(b[0], b[1], banks[count % 4])
+            count += 1
+        total(4, 6)
+        for i, b in enumerate(fourth):
+            if i == 2:
+                spread_and_store(4, 6)
+            sum_differences(b[0], b[1], banks[count % 4])
+            count += 1
+        total(6, 8)
+        spread_and_store(6, 8)

@@ -46,17 +46,25 @@ def tile_dispatcher_pa_t_kernel(tc, inv, Wk_words, Wk_scales, bk, out):
         psum = stack.enter_context(tc.psum_pool(name="psum", bufs=2))
         stack.enter_context(tc.manual_schedule())
 
+        x_tiles = []
+        for t in range(2):
+            x_single = keep.tile([P, D], BF16, name="x_single%d" % t)
+            x_tiles.append(x_single[:])
         x_pairs = []
-        for s in range(ROUNDS // 2):
+        for s in range(1, ROUNDS // 2):
             x_pair = keep.tile([P, 2, D], BF16, name="x_pair%d" % s)
             x_pairs.append(x_pair)
+            x_tiles.extend([x_pair[:, 0, :], x_pair[:, 1, :]])
         w_words = keep.tile([P, PASSES, 2 * D], U8, name="w_words", align_bytes=64)
         w_planes = keep.tile([P, PASSES, D], U8, name="w_planes", align_bytes=64)
         bias = keep.tile([P, D], BF16, name="bias")
 
+        bias_row = keep.tile([P, D], BF16, name="bias_row")
+        ones = keep.tile([P, P], BF16, name="ones")
         nc.vector.memset(w_planes[:].bitcast(I32), 0)
-        nc.scalar.dma_start(out=bias[:], in_=bk.partition_broadcast(P))
-        nc.sync.dma_start(out=x_pairs[0][:], in_=by_partition[:, 0:2, :])
+        nc.vector.memset(bias_row[:], 0.0)
+        nc.vector.memset(ones[:], 1.0)
+        nc.sync.dma_start(out=x_tiles[0], in_=by_partition[:, 0, :])
         nc.sync.dma_start(
             out=w_words[:].bitcast(I32), in_=Wk_words.rearrange("g p b -> p g b").bitcast(I32)
         )
@@ -65,8 +73,10 @@ def tile_dispatcher_pa_t_kernel(tc, inv, Wk_words, Wk_scales, bk, out):
                 out=w_planes[32 * quadrant : 32 * quadrant + 4, :, :].bitcast(I32),
                 in_=Wk_scales[:, 4 * quadrant : 4 * quadrant + 4, :].rearrange("g r n -> r g n").bitcast(I32),
             )
+        nc.sync.dma_start(out=bias_row[0:1, :], in_=bk.rearrange("(o n) -> o n", o=1))
+        nc.sync.dma_start(out=x_tiles[1], in_=by_partition[:, 1, :])
         for s in range(1, ROUNDS // 2):
-            nc.sync.dma_start(out=x_pairs[s][:], in_=by_partition[:, 2 * s : 2 * s + 2, :])
+            nc.sync.dma_start(out=x_pairs[s - 1][:], in_=by_partition[:, 2 * s : 2 * s + 2, :])
 
         ident = keep.tile([P, P], F32, name="ident")
         make_identity(nc, ident[:])
@@ -89,8 +99,7 @@ def tile_dispatcher_pa_t_kernel(tc, inv, Wk_words, Wk_scales, bk, out):
         grouped, codes, planes, acc, lin, clamped, signed = {}, {}, {}, {}, {}, {}, {}
 
         def turn_tokens(t):
-            x_tile = x_pairs[t // 2][:, t % 2, :]
-            x_words = x_tile.bitcast(F32)
+            x_words = x_tiles[t].bitcast(F32)
             xt = psum.tile([P, 2 * PASSES, P], F32, name="xt")
             for g in range(PASSES):
                 for u in range(2):
@@ -101,6 +110,14 @@ def tile_dispatcher_pa_t_kernel(tc, inv, Wk_words, Wk_scales, bk, out):
             nc.scalar.copy(
                 out=grouped[t][:].bitcast(F32), in_=xt[:].rearrange("p (g u) r -> p g r u", u=2)
             )
+
+        def spread_bias():
+            for h in range(HALVES):
+                repeated = psum.tile([P, BANK], F32, name="acc%d" % h)
+                nc.tensor.matmul(
+                    out=repeated[:], lhsT=ones[:], rhs=bias_row[:, BANK * h : BANK * (h + 1)], start=True, stop=True
+                )
+                nc.vector.tensor_copy(out=bias[:, BANK * h : BANK * (h + 1)], in_=repeated[:])
 
         def quantise(t):
             codes[t] = stage.tile([P, PASSES * P], U32, name="codes", align_bytes=64)
@@ -200,6 +217,8 @@ def tile_dispatcher_pa_t_kernel(tc, inv, Wk_words, Wk_scales, bk, out):
         for k in range(TILES + 3):
             if k < TILES:
                 turn_tokens(k)
+            if k == 0:
+                spread_bias()
             if 0 <= k - 1 < TILES:
                 quantise(k - 1)
                 multiply(k - 1)

@@ -41,8 +41,7 @@ def tile_dispatcher_pa_t_kernel(tc, inv, Wk_words, Wk_scales, bk, out):
         keep = stack.enter_context(tc.tile_pool(name="keep", bufs=1))
         stage = stack.enter_context(tc.tile_pool(name="stage", bufs=3))
         waste = stack.enter_context(tc.tile_pool(name="waste", bufs=2))
-        waiting = stack.enter_context(tc.tile_pool(name="waiting", bufs=3))
-        turning = stack.enter_context(tc.tile_pool(name="turning", bufs=20))
+        turning = stack.enter_context(tc.tile_pool(name="turning", bufs=22))
         psum = stack.enter_context(tc.psum_pool(name="psum", bufs=2))
         stack.enter_context(tc.manual_schedule())
 
@@ -61,10 +60,11 @@ def tile_dispatcher_pa_t_kernel(tc, inv, Wk_words, Wk_scales, bk, out):
 
         bias_row = keep.tile([P, D], BF16, name="bias_row")
         ones = keep.tile([P, P], BF16, name="ones")
-        nc.vector.memset(w_planes[:].bitcast(I32), 0)
         nc.vector.memset(bias_row[:], 0.0)
         nc.vector.memset(ones[:], 1.0)
+        nc.vector.memset(w_planes[:].bitcast(I32), 0)
         nc.sync.dma_start(out=x_tiles[0], in_=by_partition[:, 0, :])
+        nc.sync.dma_start(out=bias_row[0:1, :], in_=bk.rearrange("(o n) -> o n", o=1))
         nc.sync.dma_start(
             out=w_words[:].bitcast(I32), in_=Wk_words.rearrange("g p b -> p g b").bitcast(I32)
         )
@@ -73,7 +73,6 @@ def tile_dispatcher_pa_t_kernel(tc, inv, Wk_words, Wk_scales, bk, out):
                 out=w_planes[32 * quadrant : 32 * quadrant + 4, :, :].bitcast(I32),
                 in_=Wk_scales[:, 4 * quadrant : 4 * quadrant + 4, :].rearrange("g r n -> r g n").bitcast(I32),
             )
-        nc.sync.dma_start(out=bias_row[0:1, :], in_=bk.rearrange("(o n) -> o n", o=1))
         nc.sync.dma_start(out=x_tiles[1], in_=by_partition[:, 1, :])
         for s in range(1, ROUNDS // 2):
             nc.sync.dma_start(out=x_pairs[s - 1][:], in_=by_partition[:, 2 * s : 2 * s + 2, :])
@@ -96,7 +95,7 @@ def tile_dispatcher_pa_t_kernel(tc, inv, Wk_words, Wk_scales, bk, out):
         groups.extend([[ROUNDS - 4, ROUNDS - 3], [ROUNDS - 2, ROUNDS - 1]])
         abs_sums = keep.tile([P, D_TILES, len(groups)], F32, name="abs_sums")
 
-        grouped, codes, planes, acc, lin, clamped, signed = {}, {}, {}, {}, {}, {}, {}
+        grouped, codes, planes, acc, lin, signed = {}, {}, {}, {}, {}, {}
 
         def turn_tokens(t):
             x_words = x_tiles[t].bitcast(F32)
@@ -111,13 +110,18 @@ def tile_dispatcher_pa_t_kernel(tc, inv, Wk_words, Wk_scales, bk, out):
                 out=grouped[t][:].bitcast(F32), in_=xt[:].rearrange("p (g u) r -> p g r u", u=2)
             )
 
+        repeated = {}
+
         def spread_bias():
             for h in range(HALVES):
-                repeated = psum.tile([P, BANK], F32, name="acc%d" % h)
+                repeated[h] = psum.tile([P, BANK], F32, name="turned")
                 nc.tensor.matmul(
-                    out=repeated[:], lhsT=ones[:], rhs=bias_row[:, BANK * h : BANK * (h + 1)], start=True, stop=True
+                    out=repeated[h][:], lhsT=ones[:], rhs=bias_row[:, BANK * h : BANK * (h + 1)], start=True, stop=True
                 )
-                nc.vector.tensor_copy(out=bias[:, BANK * h : BANK * (h + 1)], in_=repeated[:])
+
+        def keep_bias():
+            for h in range(HALVES):
+                nc.vector.tensor_copy(out=bias[:, BANK * h : BANK * (h + 1)], in_=repeated[h][:])
 
         def quantise(t):
             codes[t] = stage.tile([P, PASSES * P], U32, name="codes", align_bytes=64)
@@ -156,9 +160,12 @@ def tile_dispatcher_pa_t_kernel(tc, inv, Wk_words, Wk_scales, bk, out):
                 )
 
         def clamp_and_square(t):
-            clamped[t] = waiting.tile([P, D], F32, name="clamped")
+            if t == 0:
+                signed[t] = first_signed
+            else:
+                signed[t] = turning.tile([P, D], F32, name="signed")
             nc.vector.tensor_scalar(
-                out=clamped[t][:], in0=lin[t][:], scalar1=-DELTA, scalar2=DELTA, op0=ALU.max, op1=ALU.min
+                out=signed[t][:], in0=lin[t][:], scalar1=-DELTA, scalar2=DELTA, op0=ALU.max, op1=ALU.min
             )
             squares = waste.tile([P, D], F32, name="squares")
             nc.scalar.activation(
@@ -177,14 +184,10 @@ def tile_dispatcher_pa_t_kernel(tc, inv, Wk_words, Wk_scales, bk, out):
                 op0=ALU.add, op1=ALU.mult,
             )
 
-        def scale_rows(t):
-            if t == 0:
-                signed[t] = first_signed
-            else:
-                signed[t] = turning.tile([P, D], F32, name="signed")
+        def scale_rows(t, lo, hi):
             nc.vector.tensor_scalar(
-                out=signed[t][:],
-                in0=clamped[t][:],
+                out=signed[t][:, lo:hi],
+                in0=signed[t][:, lo:hi],
                 scalar1=scales[:, t : t + 1],
                 scalar2=(1.0 if t % 2 == 0 else -1.0),
                 op0=ALU.mult,
@@ -213,7 +216,25 @@ def tile_dispatcher_pa_t_kernel(tc, inv, Wk_words, Wk_scales, bk, out):
                 accum_out=abs_sums[:, m, q : q + 1],
             )
 
-        first_line, second_line = [], []
+        plan, first_line, second_line = [], [], []
+        for k in range(TILES + 3):
+            for q in range(len(groups)):
+                if min(groups[q][-1] + 1, TILES - 1) == k - 3:
+                    first_line.extend([(q, m) for m in range(0, D_TILES // 2)])
+                    second_line.extend([(q, m) for m in range(D_TILES // 2, D_TILES)])
+            taken = (first_line + second_line)[0 : 2 - k % 2]
+            second_line = second_line[max(0, len(taken) - len(first_line)) :]
+            first_line = first_line[len(taken) :]
+            plan.append(taken)
+        whole = set()
+        for taken in plan:
+            for q, m in taken:
+                if m >= D_TILES // 2:
+                    for j in groups[q]:
+                        whole.add(j)
+                        whole.add((j + 1) % TILES)
+        late = [t for t in range(TILES) if t not in whole]
+
         for k in range(TILES + 3):
             if k < TILES:
                 turn_tokens(k)
@@ -222,23 +243,16 @@ def tile_dispatcher_pa_t_kernel(tc, inv, Wk_words, Wk_scales, bk, out):
             if 0 <= k - 1 < TILES:
                 quantise(k - 1)
                 multiply(k - 1)
+            if k == 1:
+                keep_bias()
             if 0 <= k - 2 < TILES:
                 add_bias(k - 2)
                 clamp_and_square(k - 2)
                 row_scale(k - 2)
             if 0 <= k - 3 < TILES:
-                scale_rows(k - 3)
-                for q in range(len(groups)):
-                    if min(groups[q][-1] + 1, TILES - 1) == k - 3:
-                        first_line.extend([(q, m) for m in range(0, D_TILES // 2)])
-                        second_line.extend([(q, m) for m in range(D_TILES // 2, D_TILES)])
-            for turn in range(2 - k % 2):
-                if first_line:
-                    sum_differences(*first_line[0])
-                    first_line = first_line[1:]
-                elif second_line:
-                    sum_differences(*second_line[0])
-                    second_line = second_line[1:]
+                scale_rows(k - 3, 0, D if k - 3 in whole else D // 2)
+            for q, m in plan[k]:
+                sum_differences(q, m)
 
         diff_t = keep.tile([P, D_TILES], F32, name="diff_t")
         loss_rows = keep.tile([P, D], F32, name="loss_rows")
@@ -252,7 +266,7 @@ def tile_dispatcher_pa_t_kernel(tc, inv, Wk_words, Wk_scales, bk, out):
                 nc.tensor.transpose(
                     spread[:, (m - m0) * P : (m - m0 + 1) * P], diff_t[:, m : m + 1].to_broadcast([P, P]), ident[:]
                 )
-            nc.vector.tensor_copy(out=loss_rows[:, m0 * P : m1 * P], in_=spread[:, 0 : (m1 - m0) * P])
+            nc.scalar.copy(out=loss_rows[:, m0 * P : m1 * P], in_=spread[:, 0 : (m1 - m0) * P])
             for a in range(D // P):
                 nc.sync.dma_start(out=out[a * P : (a + 1) * P, m0 * P : m1 * P], in_=loss_rows[:, m0 * P : m1 * P])
 
@@ -261,7 +275,11 @@ def tile_dispatcher_pa_t_kernel(tc, inv, Wk_words, Wk_scales, bk, out):
         for q, m in first_line:
             sum_differences(q, m, banks[count % 4])
             count += 1
+        for t in late[0:6]:
+            scale_rows(t, D // 2, D)
         total(0, 4)
+        for t in late[6:]:
+            scale_rows(t, D // 2, D)
         third = [b for b in second_line if b[1] < 6]
         fourth = [b for b in second_line if b[1] >= 6]
         for i, b in enumerate(third):

@@ -26,6 +26,7 @@ ROUNDS = TOKENS // P
 TILES = ROUNDS
 D_TILES = D // P
 GROUP = BANK // P
+AHEAD = 4
 EPS = 1e-8
 DELTA = EPS / math.sqrt(D)
 
@@ -40,6 +41,7 @@ def tile_dispatcher_pa_t_kernel(tc, inv, Wk_words, Wk_scales, bk, out):
     with ExitStack() as stack:
         keep = stack.enter_context(tc.tile_pool(name="keep", bufs=1))
         stage = stack.enter_context(tc.tile_pool(name="stage", bufs=3))
+        ready = stack.enter_context(tc.tile_pool(name="ready", bufs=AHEAD + 2))
         waste = stack.enter_context(tc.tile_pool(name="waste", bufs=2))
         turning = stack.enter_context(tc.tile_pool(name="turning", bufs=22))
         psum = stack.enter_context(tc.psum_pool(name="psum", bufs=2))
@@ -105,7 +107,7 @@ def tile_dispatcher_pa_t_kernel(tc, inv, Wk_words, Wk_scales, bk, out):
                     nc.tensor.transpose(
                         xt[:, 2 * g + u, :], x_words[:, 256 * g + u : 256 * (g + 1) : 2], ident[:]
                     )
-            grouped[t] = stage.tile([P, PASSES, P, 4], BF16, name="grouped", align_bytes=64)
+            grouped[t] = ready.tile([P, PASSES, P, 4], BF16, name="grouped", align_bytes=64)
             nc.scalar.copy(
                 out=grouped[t][:].bitcast(F32), in_=xt[:].rearrange("p (g u) r -> p g r u", u=2)
             )
@@ -175,21 +177,21 @@ def tile_dispatcher_pa_t_kernel(tc, inv, Wk_words, Wk_scales, bk, out):
         def row_scale(t):
             col = slice(t, t + 1)
             nc.gpsimd.tensor_scalar(
+                out=scales[:, col], in0=row_sums[:, 0, col], scalar1=row_sums[:, 1, col],
+                scalar2=(1.0 if t % 2 == 0 else -1.0), op0=ALU.add, op1=ALU.mult,
+            )
+            nc.gpsimd.tensor_scalar(
                 out=floored[:, col], in0=norm_sq[:, col], scalar1=EPS * EPS, scalar2=EPS * EPS,
                 op0=ALU.max, op1=ALU.mult,
             )
             nc.gpsimd.tensor_tensor(out=inv_norm[:, col], in0=floored[:, col], in1=neg_half[:], op=ALU.pow)
-            nc.gpsimd.tensor_scalar(
-                out=scales[:, col], in0=row_sums[:, 0, col], scalar1=row_sums[:, 1, col], scalar2=inv_norm[:, col],
-                op0=ALU.add, op1=ALU.mult,
-            )
 
         def scale_rows(t, lo, hi):
             nc.vector.tensor_scalar(
                 out=signed[t][:, lo:hi],
                 in0=signed[t][:, lo:hi],
-                scalar1=scales[:, t : t + 1],
-                scalar2=(1.0 if t % 2 == 0 else -1.0),
+                scalar1=inv_norm[:, t : t + 1],
+                scalar2=scales[:, t : t + 1],
                 op0=ALU.mult,
                 op1=ALU.mult,
             )
@@ -235,9 +237,12 @@ def tile_dispatcher_pa_t_kernel(tc, inv, Wk_words, Wk_scales, bk, out):
                         whole.add((j + 1) % TILES)
         late = [t for t in range(TILES) if t not in whole]
 
+        def turned_after(k):
+            return min(TILES, k + 1 + max(0, min(k - 2, AHEAD)))
+
         for k in range(TILES + 3):
-            if k < TILES:
-                turn_tokens(k)
+            for t in range(turned_after(k - 1), turned_after(k)):
+                turn_tokens(t)
             if k == 0:
                 spread_bias()
             if 0 <= k - 1 < TILES:
@@ -249,6 +254,9 @@ def tile_dispatcher_pa_t_kernel(tc, inv, Wk_words, Wk_scales, bk, out):
                 add_bias(k - 2)
                 clamp_and_square(k - 2)
                 row_scale(k - 2)
+            if k - 3 == TILES - 1:
+                for t in late[0:5]:
+                    scale_rows(t, D // 2, D)
             if 0 <= k - 3 < TILES:
                 scale_rows(k - 3, 0, D if k - 3 in whole else D // 2)
             for q, m in plan[k]:
@@ -275,15 +283,16 @@ def tile_dispatcher_pa_t_kernel(tc, inv, Wk_words, Wk_scales, bk, out):
         for q, m in first_line:
             sum_differences(q, m, banks[count % 4])
             count += 1
-        for t in late[0:6]:
+        for t in late[5:8]:
             scale_rows(t, D // 2, D)
         total(0, 4)
-        for t in late[6:]:
+        for t in late[8:]:
             scale_rows(t, D // 2, D)
         third = [b for b in second_line if b[1] < 6]
-        fourth = [b for b in second_line if b[1] >= 6]
+        fourth = [b for b in second_line if b[1] == 6]
+        fifth = [b for b in second_line if b[1] == 7]
         for i, b in enumerate(third):
-            if i == 2:
+            if i == 1:
                 spread_and_store(0, 4)
             sum_differences(b[0], b[1], banks[count % 4])
             count += 1
@@ -293,5 +302,11 @@ def tile_dispatcher_pa_t_kernel(tc, inv, Wk_words, Wk_scales, bk, out):
                 spread_and_store(4, 6)
             sum_differences(b[0], b[1], banks[count % 4])
             count += 1
-        total(6, 8)
-        spread_and_store(6, 8)
+        total(6, 7)
+        for i, b in enumerate(fifth):
+            if i == 2:
+                spread_and_store(6, 7)
+            sum_differences(b[0], b[1], banks[count % 4])
+            count += 1
+        total(7, 8)
+        spread_and_store(7, 8)

@@ -161,17 +161,19 @@ def tile_dispatcher_pa_t_kernel(tc, inv, Wk_words, Wk_scales, bk, out):
                     accum_out=row_sums[:, h, t : t + 1],
                 )
 
-        def clamp_and_square(t):
+        def square(t):
+            squares = waste.tile([P, D], F32, name="squares")
+            nc.scalar.activation(
+                out=squares[:], in_=lin[t][:], func=ACT.Square, accum_out=norm_sq[:, t : t + 1]
+            )
+
+        def clamp(t):
             if t == 0:
                 signed[t] = first_signed
             else:
                 signed[t] = turning.tile([P, D], F32, name="signed")
             nc.vector.tensor_scalar(
                 out=signed[t][:], in0=lin[t][:], scalar1=-DELTA, scalar2=DELTA, op0=ALU.max, op1=ALU.min
-            )
-            squares = waste.tile([P, D], F32, name="squares")
-            nc.scalar.activation(
-                out=squares[:], in_=lin[t][:], func=ACT.Square, accum_out=norm_sq[:, t : t + 1]
             )
 
         def row_scale(t):
@@ -218,10 +220,16 @@ def tile_dispatcher_pa_t_kernel(tc, inv, Wk_words, Wk_scales, bk, out):
                 accum_out=abs_sums[:, m, q : q + 1],
             )
 
+        def clamped_in(t):
+            return min(t + 3, TILES + 1)
+
+        def scaled_in(t):
+            return min(t + 4, TILES + 2)
+
         plan, first_line, second_line = [], [], []
         for k in range(TILES + 3):
             for q in range(len(groups)):
-                if min(groups[q][-1] + 1, TILES - 1) == k - 3:
+                if scaled_in(min(groups[q][-1] + 1, TILES - 1)) == k:
                     first_line.extend([(q, m) for m in range(0, D_TILES // 2)])
                     second_line.extend([(q, m) for m in range(D_TILES // 2, D_TILES)])
             taken = (first_line + second_line)[0 : 2 - k % 2]
@@ -252,13 +260,17 @@ def tile_dispatcher_pa_t_kernel(tc, inv, Wk_words, Wk_scales, bk, out):
                 keep_bias()
             if 0 <= k - 2 < TILES:
                 add_bias(k - 2)
-                clamp_and_square(k - 2)
+                square(k - 2)
                 row_scale(k - 2)
-            if k - 3 == TILES - 1:
-                for t in late[0:5]:
-                    scale_rows(t, D // 2, D)
-            if 0 <= k - 3 < TILES:
-                scale_rows(k - 3, 0, D if k - 3 in whole else D // 2)
+            for t in range(TILES):
+                if clamped_in(t) == k:
+                    clamp(t)
+            for t in range(TILES):
+                if scaled_in(t) == k:
+                    if t == TILES - 1:
+                        for u in late[0:5]:
+                            scale_rows(u, D // 2, D)
+                    scale_rows(t, 0, D if t in whole else D // 2)
             for q, m in plan[k]:
                 sum_differences(q, m)
 

@@ -85,13 +85,11 @@ def tile_dispatcher_pa_t_kernel(tc, inv, Wk_words, Wk_scales, bk, out):
         nc.vector.tensor_copy(out=next_row[:, 0 : P - 1], in_=ident[:, 1:P])
         nc.vector.tensor_copy(out=next_row[:, P - 1 : P], in_=ident[:, 0:1])
         first_signed = keep.tile([P, D], F32, name="first_signed")
-        neg_half = keep.tile([P, 1], F32, name="neg_half")
-        nc.gpsimd.memset(neg_half[:], -0.5)
 
         row_sums = keep.tile([P, HALVES, TILES], F32, name="row_sums")
         norm_sq = keep.tile([P, TILES], F32, name="norm_sq")
-        floored = keep.tile([P, TILES], F32, name="floored")
         inv_norm = keep.tile([P, TILES], F32, name="inv_norm")
+        floored = keep.tile([P, TILES], F32, name="floored")
         scales = keep.tile([P, TILES], F32, name="scales")
         groups = [list(range(j, j + GROUP)) for j in range(0, ROUNDS - GROUP, GROUP)]
         groups.extend([[ROUNDS - 4, ROUNDS - 3], [ROUNDS - 2, ROUNDS - 1]])
@@ -186,7 +184,10 @@ def tile_dispatcher_pa_t_kernel(tc, inv, Wk_words, Wk_scales, bk, out):
                 out=floored[:, col], in0=norm_sq[:, col], scalar1=EPS * EPS, scalar2=EPS * EPS,
                 op0=ALU.max, op1=ALU.mult,
             )
-            nc.gpsimd.tensor_tensor(out=inv_norm[:, col], in0=floored[:, col], in1=neg_half[:], op=ALU.pow)
+
+        def invert_norm(t):
+            col = slice(t, t + 1)
+            nc.scalar.activation(out=inv_norm[:, col], in_=floored[:, col], func=ACT.Abs_reciprocal_sqrt)
 
         def scale_rows(t, lo, hi):
             nc.vector.tensor_scalar(
@@ -258,6 +259,8 @@ def tile_dispatcher_pa_t_kernel(tc, inv, Wk_words, Wk_scales, bk, out):
                 multiply(k - 1)
             if k == 1:
                 keep_bias()
+            if 0 <= k - 3 < TILES:
+                invert_norm(k - 3)
             if 0 <= k - 2 < TILES:
                 add_bias(k - 2)
                 square(k - 2)

@@ -62,19 +62,19 @@ def tile_dispatcher_pa_t_kernel(tc, inv, Wk_words, Wk_scales, bk, out):
 
         bias_row = keep.tile([P, D], BF16, name="bias_row")
         ones = keep.tile([P, P], BF16, name="ones")
+        nc.vector.memset(w_planes[:].bitcast(I32), 0)
         nc.vector.memset(bias_row[:], 0.0)
         nc.vector.memset(ones[:], 1.0)
-        nc.vector.memset(w_planes[:].bitcast(I32), 0)
         nc.sync.dma_start(out=x_tiles[0], in_=by_partition[:, 0, :])
-        nc.sync.dma_start(out=bias_row[0:1, :], in_=bk.rearrange("(o n) -> o n", o=1))
+        for r in range(4):
+            nc.sync.dma_start(
+                out=w_planes[r : P : 32, :, :].bitcast(I32),
+                in_=Wk_scales[:, r : 16 : 4, :].rearrange("g q n -> q g n").bitcast(I32),
+            )
         nc.sync.dma_start(
             out=w_words[:].bitcast(I32), in_=Wk_words.rearrange("g p b -> p g b").bitcast(I32)
         )
-        for quadrant in range(4):
-            nc.sync.dma_start(
-                out=w_planes[32 * quadrant : 32 * quadrant + 4, :, :].bitcast(I32),
-                in_=Wk_scales[:, 4 * quadrant : 4 * quadrant + 4, :].rearrange("g r n -> r g n").bitcast(I32),
-            )
+        nc.sync.dma_start(out=bias_row[0:1, :], in_=bk.rearrange("(o n) -> o n", o=1))
         nc.sync.dma_start(out=x_tiles[1], in_=by_partition[:, 1, :])
         for s in range(1, ROUNDS // 2):
             nc.sync.dma_start(out=x_pairs[s - 1][:], in_=by_partition[:, 2 * s : 2 * s + 2, :])

@@ -26,7 +26,7 @@ ROUNDS = TOKENS // P
 TILES = ROUNDS
 D_TILES = D // P
 GROUP = BANK // P
-AHEAD = 4
+AHEAD = 6
 EPS = 1e-8
 DELTA = EPS / math.sqrt(D)
 
@@ -65,7 +65,11 @@ def tile_dispatcher_pa_t_kernel(tc, inv, Wk_words, Wk_scales, bk, out):
         nc.vector.memset(w_planes[:].bitcast(I32), 0)
         nc.vector.memset(bias_row[:], 0.0)
         nc.vector.memset(ones[:], 1.0)
+        first_column = keep.tile([P, 1], F32, name="first_column")
+        nc.scalar.activation(out=first_column[:], in_=ones[:, 0:1], func=ACT.Abs_reciprocal_sqrt)
         nc.sync.dma_start(out=x_tiles[0], in_=by_partition[:, 0, :])
+        nc.sync.dma_start(out=x_tiles[1], in_=by_partition[:, 1, :])
+        nc.sync.dma_start(out=bias_row[0:1, :], in_=bk.rearrange("(o n) -> o n", o=1))
         for r in range(4):
             nc.sync.dma_start(
                 out=w_planes[r : P : 32, :, :].bitcast(I32),
@@ -74,8 +78,6 @@ def tile_dispatcher_pa_t_kernel(tc, inv, Wk_words, Wk_scales, bk, out):
         nc.sync.dma_start(
             out=w_words[:].bitcast(I32), in_=Wk_words.rearrange("g p b -> p g b").bitcast(I32)
         )
-        nc.sync.dma_start(out=bias_row[0:1, :], in_=bk.rearrange("(o n) -> o n", o=1))
-        nc.sync.dma_start(out=x_tiles[1], in_=by_partition[:, 1, :])
         for s in range(1, ROUNDS // 2):
             nc.sync.dma_start(out=x_pairs[s - 1][:], in_=by_partition[:, 2 * s : 2 * s + 2, :])
 
@@ -233,7 +235,7 @@ def tile_dispatcher_pa_t_kernel(tc, inv, Wk_words, Wk_scales, bk, out):
                 if scaled_in(min(groups[q][-1] + 1, TILES - 1)) == k:
                     first_line.extend([(q, m) for m in range(0, D_TILES // 2)])
                     second_line.extend([(q, m) for m in range(D_TILES // 2, D_TILES)])
-            taken = (first_line + second_line)[0 : 2 - k % 2]
+            taken = (first_line + second_line)[0 : (2 if k % GROUP in (0, GROUP - 1) else 1)]
             second_line = second_line[max(0, len(taken) - len(first_line)) :]
             first_line = first_line[len(taken) :]
             plan.append(taken)
@@ -252,7 +254,7 @@ def tile_dispatcher_pa_t_kernel(tc, inv, Wk_words, Wk_scales, bk, out):
         for k in range(TILES + 3):
             for t in range(turned_after(k - 1), turned_after(k)):
                 turn_tokens(t)
-            if k == 0:
+            if k == 1:
                 spread_bias()
             if 0 <= k - 1 < TILES:
                 quantise(k - 1)

@@ -26,7 +26,7 @@ ROUNDS = TOKENS // P
 TILES = ROUNDS
 D_TILES = D // P
 GROUP = BANK // P
-AHEAD = 6
+AHEAD = 8
 EPS = 1e-8
 DELTA = EPS / math.sqrt(D)
 
@@ -273,7 +273,7 @@ def tile_dispatcher_pa_t_kernel(tc, inv, Wk_words, Wk_scales, bk, out):
             for t in range(TILES):
                 if scaled_in(t) == k:
                     if t == TILES - 1:
-                        for u in late[0:5]:
+                        for u in late[0:3]:
                             scale_rows(u, D // 2, D)
                     scale_rows(t, 0, D if t in whole else D // 2)
             for q, m in plan[k]:
@@ -300,7 +300,7 @@ def tile_dispatcher_pa_t_kernel(tc, inv, Wk_words, Wk_scales, bk, out):
         for q, m in first_line:
             sum_differences(q, m, banks[count % 4])
             count += 1
-        for t in late[5:8]:
+        for t in late[3:8]:
             scale_rows(t, D // 2, D)
         total(0, 4)
         for t in late[8:]:

import math
from contextlib import ExitStack

import concourse.mybir as mybir
from concourse.masks import make_identity

F32 = mybir.dt.float32
BF16 = mybir.dt.bfloat16
U8 = mybir.dt.uint8
U32 = mybir.dt.uint32
I32 = mybir.dt.int32
FP8X4 = mybir.dt.float8_e4m3fn_x4
FP4X4 = mybir.dt.float4_e2m1fn_x4
ALU = mybir.AluOpType
ACT = mybir.ActivationFunctionType
AXIS = mybir.AxisListType

P = 128
TOKENS = 4096
D = 1024
K_PASS = 4 * P
PASSES = D // K_PASS
BANK = 512
HALVES = D // BANK
ROUNDS = TOKENS // P
TILES = ROUNDS
D_TILES = D // P
GROUP = BANK // P
AHEAD = 8
EPS = 1e-8
DELTA = EPS / math.sqrt(D)

FLOPS = 2 * TOKENS * D * D


def tile_dispatcher_pa_t_kernel(tc, inv, Wk_words, Wk_scales, bk, out):
    nc = tc.nc
    flat = inv.flatten_outer_dims()
    by_partition = flat.rearrange("(p t) k -> p t k", t=ROUNDS)

    with ExitStack() as stack:
        keep = stack.enter_context(tc.tile_pool(name="keep", bufs=1))
        stage = stack.enter_context(tc.tile_pool(name="stage", bufs=3))
        ready = stack.enter_context(tc.tile_pool(name="ready", bufs=AHEAD + 2))
        waste = stack.enter_context(tc.tile_pool(name="waste", bufs=2))
        turning = stack.enter_context(tc.tile_pool(name="turning", bufs=22))
        psum = stack.enter_context(tc.psum_pool(name="psum", bufs=2))
        stack.enter_context(tc.manual_schedule())

        x_tiles = []
        for t in range(2):
            x_single = keep.tile([P, D], BF16, name="x_single%d" % t)
            x_tiles.append(x_single[:])
        x_pairs = []
        for s in range(1, ROUNDS // 2):
            x_pair = keep.tile([P, 2, D], BF16, name="x_pair%d" % s)
            x_pairs.append(x_pair)
            x_tiles.extend([x_pair[:, 0, :], x_pair[:, 1, :]])
        w_words = keep.tile([P, PASSES, 2 * D], U8, name="w_words", align_bytes=64)
        w_planes = keep.tile([P, PASSES, D], U8, name="w_planes", align_bytes=64)
        bias = keep.tile([P, D], BF16, name="bias")

        bias_row = keep.tile([P, D], BF16, name="bias_row")
        ones = keep.tile([P, P], BF16, name="ones")
        nc.vector.memset(w_planes[:].bitcast(I32), 0)
        nc.vector.memset(bias_row[:], 0.0)
        nc.vector.memset(ones[:], 1.0)
        first_column = keep.tile([P, 1], F32, name="first_column")
        nc.scalar.activation(out=first_column[:], in_=ones[:, 0:1], func=ACT.Abs_reciprocal_sqrt)
        nc.sync.dma_start(out=x_tiles[0], in_=by_partition[:, 0, :])
        nc.sync.dma_start(out=x_tiles[1], in_=by_partition[:, 1, :])
        nc.sync.dma_start(out=bias_row[0:1, :], in_=bk.rearrange("(o n) -> o n", o=1))
        for r in range(4):
            nc.sync.dma_start(
                out=w_planes[r : P : 32, :, :].bitcast(I32),
                in_=Wk_scales[:, r : 16 : 4, :].rearrange("g q n -> q g n").bitcast(I32),
            )
        nc.sync.dma_start(
            out=w_words[:].bitcast(I32), in_=Wk_words.rearrange("g p b -> p g b").bitcast(I32)
        )
        for s in range(1, ROUNDS // 2):
            nc.sync.dma_start(out=x_pairs[s - 1][:], in_=by_partition[:, 2 * s : 2 * s + 2, :])

        ident = keep.tile([P, P], F32, name="ident")
        make_identity(nc, ident[:])
        next_row = keep.tile([P, P], F32, name="next_row")
        nc.vector.tensor_copy(out=next_row[:, 0 : P - 1], in_=ident[:, 1:P])
        nc.vector.tensor_copy(out=next_row[:, P - 1 : P], in_=ident[:, 0:1])
        first_signed = keep.tile([P, D], F32, name="first_signed")

        row_sums = keep.tile([P, HALVES, TILES], F32, name="row_sums")
        norm_sq = keep.tile([P, TILES], F32, name="norm_sq")
        inv_norm = keep.tile([P, TILES], F32, name="inv_norm")
        floored = keep.tile([P, TILES], F32, name="floored")
        scales = keep.tile([P, TILES], F32, name="scales")
        groups = [list(range(j, j + GROUP)) for j in range(0, ROUNDS - GROUP, GROUP)]
        groups.extend([[ROUNDS - 4, ROUNDS - 3], [ROUNDS - 2, ROUNDS - 1]])
        abs_sums = keep.tile([P, D_TILES, len(groups)], F32, name="abs_sums")

        grouped, codes, planes, acc, lin, signed = {}, {}, {}, {}, {}, {}

        def turn_tokens(t):
            x_words = x_tiles[t].bitcast(F32)
            xt = psum.tile([P, 2 * PASSES, P], F32, name="xt")
            for g in range(PASSES):
                for u in range(2):
                    nc.tensor.transpose(
                        xt[:, 2 * g + u, :], x_words[:, 256 * g + u : 256 * (g + 1) : 2], ident[:]
                    )
            grouped[t] = ready.tile([P, PASSES, P, 4], BF16, name="grouped", align_bytes=64)
            nc.scalar.copy(
                out=grouped[t][:].bitcast(F32), in_=xt[:].rearrange("p (g u) r -> p g r u", u=2)
            )

        repeated = {}

        def spread_bias():
            for h in range(HALVES):
                repeated[h] = psum.tile([P, BANK], F32, name="turned")
                nc.tensor.matmul(
                    out=repeated[h][:], lhsT=ones[:], rhs=bias_row[:, BANK * h : BANK * (h + 1)], start=True, stop=True
                )

        def keep_bias():
            for h in range(HALVES):
                nc.vector.tensor_copy(out=bias[:, BANK * h : BANK * (h + 1)], in_=repeated[h][:])

        def quantise(t):
            codes[t] = stage.tile([P, PASSES * P], U32, name="codes", align_bytes=64)
            planes[t] = stage.tile([P, PASSES * P], U8, name="planes", align_bytes=64)
            nc.vector.quantize_mx(
                out=codes[t][:].bitcast(FP8X4),
                scales=planes[t][:],
                in_=grouped[t][:].rearrange("p g r t -> p (g r t)"),
            )

        def multiply(t):
            for h in range(HALVES):
                acc[t, h] = psum.tile([P, BANK], F32, name="acc%d" % h)
                for g in range(PASSES):
                    nc.tensor.matmul_mx(
                        out=acc[t, h][:],
                        lhsT=codes[t][:, g * P : (g + 1) * P].bitcast(FP8X4),
                        lhsT_scale=planes[t][:, g * P : (g + 1) * P],
                        rhs=w_words[:, g, 2 * BANK * h : 2 * BANK * (h + 1)].bitcast(FP4X4),
                        rhs_scale=w_planes[:, g, BANK * h : BANK * (h + 1)],
                        start=(g == 0),
                        stop=(g == PASSES - 1),
                    )

        def add_bias(t):
            lin[t] = stage.tile([P, D], F32, name="lin")
            for h in range(HALVES):
                nc.vector.scalar_tensor_tensor(
                    out=lin[t][:, BANK * h : BANK * (h + 1)],
                    in0=acc[t, h][:],
                    scalar=1.0,
                    in1=bias[:, BANK * h : BANK * (h + 1)],
                    op0=ALU.mult,
                    op1=ALU.add,
                    accum_out=row_sums[:, h, t : t + 1],
                )

        def square(t):
            squares = waste.tile([P, D], F32, name="squares")
            nc.scalar.activation(
                out=squares[:], in_=lin[t][:], func=ACT.Square, accum_out=norm_sq[:, t : t + 1]
            )

        def clamp(t):
            if t == 0:
                signed[t] = first_signed
            else:
                signed[t] = turning.tile([P, D], F32, name="signed")
            nc.vector.tensor_scalar(
                out=signed[t][:], in0=lin[t][:], scalar1=-DELTA, scalar2=DELTA, op0=ALU.max, op1=ALU.min
            )

        def row_scale(t):
            col = slice(t, t + 1)
            nc.gpsimd.tensor_scalar(
                out=scales[:, col], in0=row_sums[:, 0, col], scalar1=row_sums[:, 1, col],
                scalar2=(1.0 if t % 2 == 0 else -1.0), op0=ALU.add, op1=ALU.mult,
            )
            nc.gpsimd.tensor_scalar(
                out=floored[:, col], in0=norm_sq[:, col], scalar1=EPS * EPS, scalar2=EPS * EPS,
                op0=ALU.max, op1=ALU.mult,
            )

        def invert_norm(t):
            col = slice(t, t + 1)
            nc.scalar.activation(out=inv_norm[:, col], in_=floored[:, col], func=ACT.Abs_reciprocal_sqrt)

        def scale_rows(t, lo, hi):
            nc.vector.tensor_scalar(
                out=signed[t][:, lo:hi],
                in0=signed[t][:, lo:hi],
                scalar1=inv_norm[:, t : t + 1],
                scalar2=scales[:, t : t + 1],
                op0=ALU.mult,
                op1=ALU.mult,
            )

        def sum_differences(q, m, bank="turned"):
            turned = psum.tile([P, GROUP * P], F32, name=bank)
            for i, j in enumerate(groups[q]):
                for side in range(2):
                    wraps = j + side == TILES
                    nc.tensor.matmul(
                        out=turned[:, i * P : (i + 1) * P],
                        lhsT=signed[0 if wraps else j + side][:, m * P : (m + 1) * P],
                        rhs=(next_row[:] if wraps else ident[:]),
                        is_transpose=True,
                        start=(side == 0),
                        stop=(side == 1),
                    )
            width = len(groups[q]) * P - (1 if groups[q][-1] == ROUNDS - 1 else 0)
            magnitudes = waste.tile([P, GROUP * P], F32, name="magnitudes")
            nc.scalar.activation(
                out=magnitudes[:, 0:width],
                in_=turned[:, 0:width],
                func=ACT.Abs,
                accum_out=abs_sums[:, m, q : q + 1],
            )

        def clamped_in(t):
            return min(t + 3, TILES + 1)

        def scaled_in(t):
            return min(t + 4, TILES + 2)

        plan, first_line, second_line = [], [], []
        for k in range(TILES + 3):
            for q in range(len(groups)):
                if scaled_in(min(groups[q][-1] + 1, TILES - 1)) == k:
                    first_line.extend([(q, m) for m in range(0, D_TILES // 2)])
                    second_line.extend([(q, m) for m in range(D_TILES // 2, D_TILES)])
            taken = (first_line + second_line)[0 : (2 if k % GROUP in (0, GROUP - 1) else 1)]
            second_line = second_line[max(0, len(taken) - len(first_line)) :]
            first_line = first_line[len(taken) :]
            plan.append(taken)
        whole = set()
        for taken in plan:
            for q, m in taken:
                if m >= D_TILES // 2:
                    for j in groups[q]:
                        whole.add(j)
                        whole.add((j + 1) % TILES)
        late = [t for t in range(TILES) if t not in whole]

        def turned_after(k):
            return min(TILES, k + 1 + max(0, min(k - 2, AHEAD)))

        for k in range(TILES + 3):
            for t in range(turned_after(k - 1), turned_after(k)):
                turn_tokens(t)
            if k == 1:
                spread_bias()
            if 0 <= k - 1 < TILES:
                quantise(k - 1)
                multiply(k - 1)
            if k == 1:
                keep_bias()
            if 0 <= k - 3 < TILES:
                invert_norm(k - 3)
            if 0 <= k - 2 < TILES:
                add_bias(k - 2)
                square(k - 2)
                row_scale(k - 2)
            for t in range(TILES):
                if clamped_in(t) == k:
                    clamp(t)
            for t in range(TILES):
                if scaled_in(t) == k:
                    if t == TILES - 1:
                        for u in late[0:3]:
                            scale_rows(u, D // 2, D)
                    scale_rows(t, 0, D if t in whole else D // 2)
            for q, m in plan[k]:
                sum_differences(q, m)

        diff_t = keep.tile([P, D_TILES], F32, name="diff_t")
        loss_rows = keep.tile([P, D], F32, name="loss_rows")

        def total(m0, m1):
            nc.vector.tensor_reduce(out=diff_t[:, m0:m1], in_=abs_sums[:, m0:m1, :], axis=AXIS.X, op=ALU.add)

        def spread_and_store(m0, m1):
            spread = psum.tile([P, BANK], F32, name="turned")
            for m in range(m0, m1):
                nc.tensor.transpose(
                    spread[:, (m - m0) * P : (m - m0 + 1) * P], diff_t[:, m : m + 1].to_broadcast([P, P]), ident[:]
                )
            nc.scalar.copy(out=loss_rows[:, m0 * P : m1 * P], in_=spread[:, 0 : (m1 - m0) * P])
            for a in range(D // P):
                nc.sync.dma_start(out=out[a * P : (a + 1) * P, m0 * P : m1 * P], in_=loss_rows[:, m0 * P : m1 * P])

        banks = ["xt", "acc0", "acc1", "turned"]
        count = 0
        for q, m in first_line:
            sum_differences(q, m, banks[count % 4])
            count += 1
        for t in late[3:8]:
            scale_rows(t, D // 2, D)
        total(0, 4)
        for t in late[8:]:
            scale_rows(t, D // 2, D)
        third = [b for b in second_line if b[1] < 6]
        fourth = [b for b in second_line if b[1] == 6]
        fifth = [b for b in second_line if b[1] == 7]
        for i, b in enumerate(third):
            if i == 1:
                spread_and_store(0, 4)
            sum_differences(b[0], b[1], banks[count % 4])
            count += 1
        total(4, 6)
        for i, b in enumerate(fourth):
            if i == 2:
                spread_and_store(4, 6)
            sum_differences(b[0], b[1], banks[count % 4])
            count += 1
        total(6, 7)
        for i, b in enumerate(fifth):
            if i == 2:
                spread_and_store(6, 7)
            sum_differences(b[0], b[1], banks[count % 4])
            count += 1
        total(7, 8)
        spread_and_store(7, 8)
